import numpy as np
import ml_dtypes


def mxq(x, axis, fmt="e4m3"):
    dtype, down = {"e4m3": (ml_dtypes.float8_e4m3fn, 7), "e5m2": (ml_dtypes.float8_e5m2, 14)}[fmt]
    v = np.moveaxis(np.asarray(x, np.float32).astype(ml_dtypes.bfloat16).astype(np.float64), axis, -1)
    blocks = v.reshape(v.shape[:-1] + (-1, 32))
    amax = np.abs(blocks).max(-1, keepdims=True)
    byte = np.maximum(np.where(amax > 0, np.frexp(amax)[1] - 1 + 127, 0) - down, 1)
    scale = np.exp2(byte - 127.0)
    codes = (blocks / scale).astype(np.float32).astype(dtype).astype(np.float64)
    return np.moveaxis((codes * scale).reshape(v.shape), -1, axis)


WIDE = False


def mx_kscale(k):
    if not WIDE:
        return np.ones(k)
    levels = np.array([10, -10, 5, -5, 0])
    if k % 512:
        return np.exp2(np.random.permutation(np.resize(levels, k // 32))).repeat(32)
    a = np.empty((k // 512, 16))
    for p in range(k // 512):
        a[p, :8] = np.random.permutation(np.resize(levels, 8))
        for g in range(8):
            far = levels[np.abs(levels - a[p, g]) >= 10]
            a[p, g + 8] = far[np.random.randint(len(far))]
    return np.exp2(a.ravel()).repeat(32)


BF16 = ml_dtypes.bfloat16


def bf(x):
    return np.asarray(x, np.float32).astype(BF16)


def f64(x):
    return np.asarray(x).astype(np.float64)


B, A, S, F = 128, 4, 128, 512


def setup_inputs():
    s, u = mx_kscale(F), mx_kscale(F)
    t, v = mx_kscale(F), mx_kscale(F)
    return {
        "h1": bf(np.maximum(np.random.standard_normal((B, A, F)) * 1.4, 0.0) * s),
        "W2": bf(np.random.standard_normal((A, F, F)) * 1.4 / np.sqrt(F) / s[:, None] * t),
        "b2": bf(np.random.standard_normal((A, F)) * 0.2 * t),
        "W3": bf(np.random.standard_normal((A, F, S)) / np.sqrt(F) / t[:, None]),
        "b3": bf(np.random.standard_normal((A, S)) * 0.2),
        "g1": bf(np.maximum(np.random.standard_normal((B, F)) * 1.4, 0.0) * u),
        "V2": bf(np.random.standard_normal((F, F)) * 1.4 / np.sqrt(F) / u[:, None] * v),
        "c2": bf(np.random.standard_normal(F) * 0.2 * v),
        "V3": bf(np.random.standard_normal((F, S)) / np.sqrt(F) / v[:, None]),
        "c3": bf(np.random.standard_normal(S) * 0.2),
    }


def reference(h1, W2, b2, W3, b3, g1, V2, c2, V3, c3):
    ha = mxq(f64(h1), 2, "e4m3").transpose(1, 0, 2)
    h2 = np.maximum((ha @ mxq(f64(W2), 1, "e4m3")) + f64(b2)[:, None, :], 0.0)
    psi_adv = ((mxq(h2, 2, "e4m3") @ mxq(f64(W3), 1, "e4m3")) + f64(b3)[:, None, :]).transpose(1, 0, 2)
    g2 = np.maximum((mxq(f64(g1), 1, "e4m3") @ mxq(f64(V2), 0, "e4m3")) + f64(c2), 0.0)
    psi_state = (mxq(g2, 1, "e4m3") @ mxq(f64(V3), 0, "e4m3")) + f64(c3)
    return psi_state[:, None, :] + psi_adv - psi_adv.mean(axis=1, keepdims=True)

@@ -1,0 +1,277 @@
+from contextlib import ExitStack
+
+import concourse.mybir as mybir
+from concourse.masks import make_identity
+
+F32 = mybir.dt.float32
+BF16 = mybir.dt.bfloat16
+U32 = mybir.dt.uint32
+U8 = mybir.dt.uint8
+FP8X4 = mybir.dt.float8_e4m3fn_x4
+ADD = mybir.AluOpType.add
+MULT = mybir.AluOpType.mult
+RELU = mybir.ActivationFunctionType.Relu
+
+P = 128
+PACK = 4
+B = 128
+A = 4
+F = 512
+S = 128
+NETS = A + 1
+STATE = A
+ORDER = [STATE, 0, 1, 2, 3]
+VECTOR_UNITS = 96
+SCALAR_HEADS = 2
+BLOCK = 16
+
+FLOPS = 2 * NETS * B * F * (F + S)
+
+
+def tile_psicritic_pa_s_kernel(tc, h1, W2, b2, W3, b3, g1, V2, c2, V3, c3, out):
+    nc = tc.nc
+    with ExitStack() as ctx:
+        keep = ctx.enter_context(tc.tile_pool(name="keep", bufs=1))
+        psum_three = ctx.enter_context(tc.psum_pool(name="psum_three", bufs=3))
+        psum_one = ctx.enter_context(tc.psum_pool(name="psum_one", bufs=1))
+
+        x_rows = keep.tile([P, NETS, F], BF16)
+        x_grouped = keep.tile([P, NETS, B, PACK], BF16, align_bytes=64)
+        x_codes = keep.tile([P, NETS, B], U32, align_bytes=64)
+        x_scales = keep.tile([P, NETS, B], U8, align_bytes=64)
+
+        wh_rows = keep.tile([P, NETS, PACK, F], BF16)
+        wh_grouped = keep.tile([P, NETS, PACK, P, PACK], BF16, align_bytes=64)
+        wh_codes = keep.tile([P, NETS, PACK, P], U32, align_bytes=64)
+        wh_scales = keep.tile([P, NETS, PACK, P], U8, align_bytes=64)
+
+        bh_bf16 = keep.tile([P, NETS, BLOCK], BF16)
+        bh = keep.tile([P, NETS, PACK], F32)
+
+        hid = keep.tile([P, NETS, PACK, B], BF16)
+        hid_grouped = keep.tile([P, NETS, B, PACK], BF16, align_bytes=64)
+        hid_codes = keep.tile([P, NETS, B], U32, align_bytes=64)
+        hid_scales = keep.tile([P, NETS, B], U8, align_bytes=64)
+
+        wo_rows = keep.tile([P, NETS, PACK, S], BF16)
+        wo_grouped = keep.tile([P, NETS, S, PACK], BF16, align_bytes=64)
+        wo_codes = keep.tile([P, NETS, S], U32, align_bytes=64)
+        wo_scales = keep.tile([P, NETS, S], U8, align_bytes=64)
+
+        identity = keep.tile([P, P], F32)
+        bias_rows = keep.tile([P, A, S], BF16)
+        bias_weight = keep.tile([P, P], BF16)
+        base = keep.tile([P, A, S], F32)
+        result = keep.tile([P, A, S], F32)
+
+        ctx.enter_context(tc.manual_schedule())
+
+        nc.scalar.dma_start(out=bh_bf16[:, 0:A, 0:PACK], in_=b2.rearrange("a (m j) -> m a j", j=PACK))
+        nc.scalar.dma_start(out=bh_bf16[:, STATE, 0:PACK], in_=c2.rearrange("(m j) -> m j", j=PACK))
+
+        nc.vector.memset(bias_rows[:], 0.0)
+        nc.scalar.dma_start(out=bias_rows[0:1, :, :], in_=b3.rearrange("(o a) s -> o a s", o=1))
+        nc.scalar.dma_start(
+            out=bias_rows[1:2, :, :],
+            in_=c3.rearrange("(o r s) -> o r s", o=1, r=1).to_broadcast([1, A, S]),
+        )
+        nc.scalar.dma_start(out=bias_rows[32:36, :, :], in_=b3.unsqueeze(1).to_broadcast([A, A, S]))
+        nc.vector.memset(bias_weight[:], 1.0)
+        nc.vector.memset(bias_weight[32:64, :], -1.0 / A)
+        make_identity(nc, identity[:])
+
+        def load_hidden_weights(n, w):
+            nc.sync.dma_start(
+                out=wh_rows[:, n].rearrange("q t f -> q (t f)"),
+                in_=w.rearrange("(q t) f -> q (t f)", t=PACK),
+            )
+
+        load_hidden_weights(STATE, V2)
+        load_hidden_weights(0, W2[0])
+        nc.sync.dma_start(out=x_rows[:, STATE, :], in_=g1)
+        nc.sync.dma_start(out=x_rows[:, 0:2, :], in_=h1[:, 0:2, :])
+        load_hidden_weights(1, W2[1])
+        nc.sync.dma_start(out=x_rows[:, 2:4, :], in_=h1[:, 2:4, :])
+        load_hidden_weights(2, W2[2])
+        load_hidden_weights(3, W2[3])
+        nc.sync.dma_start(
+            out=wo_rows[:, STATE].rearrange("m j s -> m (j s)"),
+            in_=V3.rearrange("(m j) s -> m (j s)", j=PACK),
+        )
+        nc.sync.dma_start(
+            out=wo_rows[:, 0:A].rearrange("m a j s -> m a (j s)"),
+            in_=W3.rearrange("a (m j) s -> m a (j s)", j=PACK),
+        )
+
+        def transpose_x(first, count):
+            xt = psum_three.tile([P, count, 2, B], F32, tag="small")
+            for i in range(count):
+                words = x_rows[:, first + i, :].bitcast(F32)
+                for u in range(2):
+                    nc.tensor.transpose(xt[:, i, u, :], words[:, u::2], identity[:])
+            nc.scalar.copy(
+                out=x_grouped[:, first : first + count]
+                .rearrange("q n r t -> q (n r t)")
+                .bitcast(F32)
+                .rearrange("q (n r u) -> q n r u", n=count, u=2),
+                in_=xt[:].rearrange("q n u r -> q n r u"),
+            )
+
+        def quantise_x(first, count):
+            nets = slice(first, first + count)
+            nc.vector.quantize_mx(
+                out=x_codes[:, nets, :].rearrange("q n r -> q (n r)").bitcast(FP8X4),
+                scales=x_scales[:, nets, :].rearrange("q n r -> q (n r)"),
+                in_=x_grouped[:, nets].rearrange("q n r t -> q (n r t)"),
+            )
+
+        def regroup_hidden_weights(n, copy, units):
+            source = wh_rows[:, n].rearrange("q t (m j) -> q m t j", j=PACK)
+            target = wh_grouped[:, n].rearrange("q j m t -> q m t j")
+            copy(out=target[:, units], in_=source[:, units])
+
+        def vector_regroups(n):
+            regroup_hidden_weights(n, nc.vector.tensor_copy, slice(0, VECTOR_UNITS))
+
+        def scalar_regroups(n):
+            regroup_hidden_weights(n, nc.scalar.copy, slice(VECTOR_UNITS, P))
+
+        def quantise_hidden_weights(n):
+            nc.vector.quantize_mx(
+                out=wh_codes[:, n].rearrange("q j m -> q (j m)").bitcast(FP8X4),
+                scales=wh_scales[:, n].rearrange("q j m -> q (j m)"),
+                in_=wh_grouped[:, n].rearrange("q j m t -> q (j m t)"),
+            )
+
+        def regroup_head_weights(n, copy):
+            copy(
+                out=wo_grouped[:, n].rearrange("m (c i) j -> m c j i", i=4),
+                in_=wo_rows[:, n].rearrange("m j (c i) -> m c j i", i=4),
+            )
+
+        def quantise_head_weights(n):
+            nc.vector.quantize_mx(
+                out=wo_codes[:, n, :].bitcast(FP8X4),
+                scales=wo_scales[:, n, :],
+                in_=wo_grouped[:, n].rearrange("m s j -> m (s j)"),
+            )
+
+        sums = {}
+
+        def hidden_passes(n):
+            acc = psum_three.tile([P, PACK, B], F32, tag="acc")
+            for j in range(PACK):
+                nc.tensor.matmul_mx(
+                    out=acc[:, j, :],
+                    lhsT=wh_codes[:, n, j, :].bitcast(FP8X4),
+                    lhsT_scale=wh_scales[:, n, j, :],
+                    rhs=x_codes[:, n, :].bitcast(FP8X4),
+                    rhs_scale=x_scales[:, n, :],
+                    start=True,
+                    stop=True,
+                )
+            sums[n] = acc
+
+        def bias_and_relu(n):
+            for j in range(PACK):
+                nc.scalar.activation(
+                    out=hid[:, n, j, :], in_=sums[n][:, j, :], func=RELU, bias=bh[:, n, j : j + 1]
+                )
+
+        def regroup_hidden(n):
+            nc.vector.tensor_copy(
+                out=hid_grouped[:, n].rearrange("m (c i) j -> m c j i", i=4),
+                in_=hid[:, n].rearrange("m j (c i) -> m c j i", i=4),
+            )
+
+        def quantise_hidden(n):
+            nc.vector.quantize_mx(
+                out=hid_codes[:, n, :].bitcast(FP8X4),
+                scales=hid_scales[:, n, :],
+                in_=hid_grouped[:, n].rearrange("m r j -> m (r j)"),
+            )
+
+        def head_pass(n, target, start, stop):
+            nc.tensor.matmul_mx(
+                out=target,
+                lhsT=hid_codes[:, n, :].bitcast(FP8X4),
+                lhsT_scale=hid_scales[:, n, :],
+                rhs=wo_codes[:, n, :].bitcast(FP8X4),
+                rhs_scale=wo_scales[:, n, :],
+                start=start,
+                stop=stop,
+            )
+
+        heads = {}
+
+        def head_passes(a):
+            head = psum_three.tile([P, S], F32, tag="small")
+            head_pass(STATE, head[:], True, False)
+            head_pass(a, head[:], False, True)
+            head_pass(a, adv_sum[:], a == 0, a == A - 1)
+            heads[a] = head
+
+        def add_head(a):
+            nc.vector.tensor_tensor(out=base[:, a, :], in0=base[:, a, :], in1=heads[a][:], op=ADD)
+
+        beta = psum_one.tile([P, A, S], F32)
+        adv_sum = psum_one.tile([P, S], F32)
+
+        vector_regroups(ORDER[0])
+        scalar_regroups(ORDER[0])
+        scalar_regroups(ORDER[1])
+        for p in range(NETS):
+            if p + 1 < NETS:
+                vector_regroups(ORDER[p + 1])
+            if p == 0:
+                transpose_x(STATE, 1)
+                nc.tensor.matmul(
+                    beta[:].rearrange("r a s -> r (a s)"),
+                    lhsT=bias_weight[:],
+                    rhs=bias_rows[:].rearrange("k a s -> k (a s)"),
+                    start=True,
+                    stop=True,
+                )
+                nc.scalar.copy(out=base[:], in_=beta[:])
+                transpose_x(0, 2)
+            if p + 2 < NETS:
+                scalar_regroups(ORDER[p + 2])
+            if p == 0:
+                transpose_x(2, 2)
+                quantise_x(STATE, 1)
+            if p == 1:
+                quantise_x(0, 2)
+            if p == 2:
+                quantise_x(2, 2)
+            quantise_hidden_weights(ORDER[p])
+            hidden_passes(ORDER[p])
+            if p == 0:
+                nc.vector.tensor_copy(out=bh[:], in_=bh_bf16[:, :, 0:PACK])
+            if 2 <= p < 2 + SCALAR_HEADS:
+                regroup_head_weights(ORDER[p - 2], nc.scalar.copy)
+            if p >= 1:
+                bias_and_relu(ORDER[p - 1])
+        bias_and_relu(ORDER[NETS - 1])
+
+        for i in range(SCALAR_HEADS, NETS):
+            regroup_head_weights(ORDER[i], nc.vector.tensor_copy)
+        for i in range(NETS):
+            regroup_hidden(ORDER[i])
+            quantise_head_weights(ORDER[i])
+            quantise_hidden(ORDER[i])
+            if i >= 1:
+                head_passes(ORDER[i])
+            if i >= 3:
+                add_head(ORDER[i - 2])
+        add_head(ORDER[NETS - 2])
+        add_head(ORDER[NETS - 1])
+
+        nc.vector.scalar_tensor_tensor(
+            out=result[:],
+            in0=adv_sum[:].unsqueeze(1).to_broadcast([P, A, S]),
+            scalar=-1.0 / A,
+            in1=base[:],
+            op0=MULT,
+            op1=ADD,
+        )
+        nc.sync.dma_start(out=out, in_=result[:])

@@ -9,8 +9,8 @@ U32 = mybir.dt.uint32
 U8 = mybir.dt.uint8
 FP8X4 = mybir.dt.float8_e4m3fn_x4
 ADD = mybir.AluOpType.add
-MULT = mybir.AluOpType.mult
 RELU = mybir.ActivationFunctionType.Relu
+COPY = mybir.ActivationFunctionType.Copy
 
 P = 128
 PACK = 4
@@ -20,9 +20,7 @@ F = 512
 S = 128
 NETS = A + 1
 STATE = A
-ORDER = [STATE, 0, 1, 2, 3]
-VECTOR_UNITS = 96
-SCALAR_HEADS = 2
+VECTOR_UNITS = 80
 BLOCK = 16
 
 FLOPS = 2 * NETS * B * F * (F + S)
@@ -32,7 +30,8 @@ def tile_psicritic_pa_s_kernel(tc, h1, W2, b2, W3, b3, g1, V2, c2, V3, c3, out):
     nc = tc.nc
     with ExitStack() as ctx:
         keep = ctx.enter_context(tc.tile_pool(name="keep", bufs=1))
-        psum_three = ctx.enter_context(tc.psum_pool(name="psum_three", bufs=3))
+        psum_small = ctx.enter_context(tc.psum_pool(name="psum_small", bufs=4))
+        psum_acc = ctx.enter_context(tc.psum_pool(name="psum_acc", bufs=2))
         psum_one = ctx.enter_context(tc.psum_pool(name="psum_one", bufs=1))
 
         x_rows = keep.tile([P, NETS, F], BF16)
@@ -45,10 +44,9 @@ def tile_psicritic_pa_s_kernel(tc, h1, W2, b2, W3, b3, g1, V2, c2, V3, c3, out):
         wh_codes = keep.tile([P, NETS, PACK, P], U32, align_bytes=64)
         wh_scales = keep.tile([P, NETS, PACK, P], U8, align_bytes=64)
 
-        bh_bf16 = keep.tile([P, NETS, BLOCK], BF16)
-        bh = keep.tile([P, NETS, PACK], F32)
+        bh = keep.tile([P, NETS, BLOCK], BF16)
 
-        hid = keep.tile([P, NETS, PACK, B], BF16)
+        hid = keep.tile([P, NETS, 2, B, 2], BF16)
         hid_grouped = keep.tile([P, NETS, B, PACK], BF16, align_bytes=64)
         hid_codes = keep.tile([P, NETS, B], U32, align_bytes=64)
         hid_scales = keep.tile([P, NETS, B], U8, align_bytes=64)
@@ -61,50 +59,63 @@ def tile_psicritic_pa_s_kernel(tc, h1, W2, b2, W3, b3, g1, V2, c2, V3, c3, out):
         identity = keep.tile([P, P], F32)
         bias_rows = keep.tile([P, A, S], BF16)
         bias_weight = keep.tile([P, P], BF16)
+        warm = keep.tile([P, 1], F32)
+        minus_mean = keep.tile([P, S], F32)
         base = keep.tile([P, A, S], F32)
         result = keep.tile([P, A, S], F32)
 
         ctx.enter_context(tc.manual_schedule())
 
-        nc.scalar.dma_start(out=bh_bf16[:, 0:A, 0:PACK], in_=b2.rearrange("a (m j) -> m a j", j=PACK))
-        nc.scalar.dma_start(out=bh_bf16[:, STATE, 0:PACK], in_=c2.rearrange("(m j) -> m j", j=PACK))
+        nc.vector.memset(warm[:], 0.0)
 
         nc.vector.memset(bias_rows[:], 0.0)
+        nc.scalar.dma_start(out=bh[:, 0:A, 0:PACK], in_=b2.rearrange("a (m j) -> m a j", j=PACK))
+        nc.scalar.dma_start(out=bh[:, STATE, 0:PACK], in_=c2.rearrange("(m j) -> m j", j=PACK))
         nc.scalar.dma_start(out=bias_rows[0:1, :, :], in_=b3.rearrange("(o a) s -> o a s", o=1))
         nc.scalar.dma_start(
             out=bias_rows[1:2, :, :],
             in_=c3.rearrange("(o r s) -> o r s", o=1, r=1).to_broadcast([1, A, S]),
         )
         nc.scalar.dma_start(out=bias_rows[32:36, :, :], in_=b3.unsqueeze(1).to_broadcast([A, A, S]))
+        nc.scalar.activation(out=warm[:], in_=warm[:], func=RELU)
         nc.vector.memset(bias_weight[:], 1.0)
         nc.vector.memset(bias_weight[32:64, :], -1.0 / A)
         make_identity(nc, identity[:])
 
-        def load_hidden_weights(n, w):
+        def load_hidden_weights(n):
             nc.sync.dma_start(
                 out=wh_rows[:, n].rearrange("q t f -> q (t f)"),
-                in_=w.rearrange("(q t) f -> q (t f)", t=PACK),
+                in_=(V2 if n == STATE else W2[n]).rearrange("(q t) f -> q (t f)", t=PACK),
             )
 
-        load_hidden_weights(STATE, V2)
-        load_hidden_weights(0, W2[0])
+        def load_head_weights(first, count):
+            nc.sync.dma_start(
+                out=wo_rows[:, first : first + count].rearrange("m a j s -> m a (j s)"),
+                in_=W3[first : first + count].rearrange("a (m j) s -> m a (j s)", j=PACK),
+            )
+
+        def load_x(first, count):
+            nc.sync.dma_start(
+                out=x_rows[:, first : first + count, :], in_=h1[:, first : first + count, :]
+            )
+
+        load_head_weights(0, 1)
+        load_head_weights(1, 3)
+        load_hidden_weights(0)
+        load_x(0, 2)
+        load_hidden_weights(1)
+        load_x(2, 2)
         nc.sync.dma_start(out=x_rows[:, STATE, :], in_=g1)
-        nc.sync.dma_start(out=x_rows[:, 0:2, :], in_=h1[:, 0:2, :])
-        load_hidden_weights(1, W2[1])
-        nc.sync.dma_start(out=x_rows[:, 2:4, :], in_=h1[:, 2:4, :])
-        load_hidden_weights(2, W2[2])
-        load_hidden_weights(3, W2[3])
+        load_hidden_weights(2)
+        load_hidden_weights(3)
         nc.sync.dma_start(
             out=wo_rows[:, STATE].rearrange("m j s -> m (j s)"),
             in_=V3.rearrange("(m j) s -> m (j s)", j=PACK),
         )
-        nc.sync.dma_start(
-            out=wo_rows[:, 0:A].rearrange("m a j s -> m a (j s)"),
-            in_=W3.rearrange("a (m j) s -> m a (j s)", j=PACK),
-        )
+        load_hidden_weights(STATE)
 
         def transpose_x(first, count):
-            xt = psum_three.tile([P, count, 2, B], F32, tag="small")
+            xt = psum_small.tile([P, count, 2, B], F32, tag="small")
             for i in range(count):
                 words = x_rows[:, first + i, :].bitcast(F32)
                 for u in range(2):
@@ -149,17 +160,18 @@ def tile_psicritic_pa_s_kernel(tc, h1, W2, b2, W3, b3, g1, V2, c2, V3, c3, out):
                 in_=wo_rows[:, n].rearrange("m j (c i) -> m c j i", i=4),
             )
 
-        def quantise_head_weights(n):
+        def quantise_head_weights(first, count):
+            nets = slice(first, first + count)
             nc.vector.quantize_mx(
-                out=wo_codes[:, n, :].bitcast(FP8X4),
-                scales=wo_scales[:, n, :],
-                in_=wo_grouped[:, n].rearrange("m s j -> m (s j)"),
+                out=wo_codes[:, nets, :].rearrange("m n s -> m (n s)").bitcast(FP8X4),
+                scales=wo_scales[:, nets, :].rearrange("m n s -> m (n s)"),
+                in_=wo_grouped[:, nets].rearrange("m n s j -> m (n s j)"),
             )
 
         sums = {}
 
         def hidden_passes(n):
-            acc = psum_three.tile([P, PACK, B], F32, tag="acc")
+            acc = psum_acc.tile([P, PACK, B], F32, tag="acc")
             for j in range(PACK):
                 nc.tensor.matmul_mx(
                     out=acc[:, j, :],
@@ -175,13 +187,16 @@ def tile_psicritic_pa_s_kernel(tc, h1, W2, b2, W3, b3, g1, V2, c2, V3, c3, out):
         def bias_and_relu(n):
             for j in range(PACK):
                 nc.scalar.activation(
-                    out=hid[:, n, j, :], in_=sums[n][:, j, :], func=RELU, bias=bh[:, n, j : j + 1]
+                    out=hid[:, n, j // 2, :, j % 2],
+                    in_=sums[n][:, j, :],
+                    func=RELU,
+                    bias=bh[:, n, j : j + 1],
                 )
 
         def regroup_hidden(n):
             nc.vector.tensor_copy(
-                out=hid_grouped[:, n].rearrange("m (c i) j -> m c j i", i=4),
-                in_=hid[:, n].rearrange("m j (c i) -> m c j i", i=4),
+                out=hid_grouped[:, n].rearrange("m r j -> m (r j)").bitcast(F32).rearrange("m (r h) -> m r h", h=2),
+                in_=hid[:, n].rearrange("m h r e -> m (h r e)").bitcast(F32).rearrange("m (h r) -> m r h", h=2),
             )
 
         def quantise_hidden(n):
@@ -202,76 +217,84 @@ def tile_psicritic_pa_s_kernel(tc, h1, W2, b2, W3, b3, g1, V2, c2, V3, c3, out):
                 stop=stop,
             )
 
+        adv_sum = psum_one.tile([P, S], F32)
+        beta = psum_one.tile([P, A, S], F32)
         heads = {}
 
-        def head_passes(a):
-            head = psum_three.tile([P, S], F32, tag="small")
-            head_pass(STATE, head[:], True, False)
-            head_pass(a, head[:], False, True)
-            head_pass(a, adv_sum[:], a == 0, a == A - 1)
+        def action_heads(a):
+            head = psum_small.tile([P, S], F32, tag="small")
             heads[a] = head
+            head_pass(a, adv_sum[:], a == 0, a == A - 1)
+            head_pass(a, heads[a][:], True, False)
 
-        def add_head(a):
-            nc.vector.tensor_tensor(out=base[:, a, :], in0=base[:, a, :], in1=heads[a][:], op=ADD)
-
-        beta = psum_one.tile([P, A, S], F32)
-        adv_sum = psum_one.tile([P, S], F32)
-
-        vector_regroups(ORDER[0])
-        scalar_regroups(ORDER[0])
-        scalar_regroups(ORDER[1])
-        for p in range(NETS):
-            if p + 1 < NETS:
-                vector_regroups(ORDER[p + 1])
-            if p == 0:
-                transpose_x(STATE, 1)
-                nc.tensor.matmul(
-                    beta[:].rearrange("r a s -> r (a s)"),
-                    lhsT=bias_weight[:],
-                    rhs=bias_rows[:].rearrange("k a s -> k (a s)"),
-                    start=True,
-                    stop=True,
-                )
-                nc.scalar.copy(out=base[:], in_=beta[:])
-                transpose_x(0, 2)
-            if p + 2 < NETS:
-                scalar_regroups(ORDER[p + 2])
-            if p == 0:
-                transpose_x(2, 2)
-                quantise_x(STATE, 1)
-            if p == 1:
-                quantise_x(0, 2)
-            if p == 2:
-                quantise_x(2, 2)
-            quantise_hidden_weights(ORDER[p])
-            hidden_passes(ORDER[p])
-            if p == 0:
-                nc.vector.tensor_copy(out=bh[:], in_=bh_bf16[:, :, 0:PACK])
-            if 2 <= p < 2 + SCALAR_HEADS:
-                regroup_head_weights(ORDER[p - 2], nc.scalar.copy)
-            if p >= 1:
-                bias_and_relu(ORDER[p - 1])
-        bias_and_relu(ORDER[NETS - 1])
-
-        for i in range(SCALAR_HEADS, NETS):
-            regroup_head_weights(ORDER[i], nc.vector.tensor_copy)
-        for i in range(NETS):
-            regroup_hidden(ORDER[i])
-            quantise_head_weights(ORDER[i])
-            quantise_hidden(ORDER[i])
-            if i >= 1:
-                head_passes(ORDER[i])
-            if i >= 3:
-                add_head(ORDER[i - 2])
-        add_head(ORDER[NETS - 2])
-        add_head(ORDER[NETS - 1])
-
-        nc.vector.scalar_tensor_tensor(
-            out=result[:],
-            in0=adv_sum[:].unsqueeze(1).to_broadcast([P, A, S]),
-            scalar=-1.0 / A,
-            in1=base[:],
-            op0=MULT,
-            op1=ADD,
+        regroup_head_weights(0, nc.vector.tensor_copy)
+        regroup_head_weights(1, nc.vector.tensor_copy)
+        regroup_head_weights(2, nc.vector.tensor_copy)
+        regroup_head_weights(3, nc.vector.tensor_copy)
+        quantise_head_weights(0, 2)
+        scalar_regroups(0)
+        vector_regroups(0)
+        quantise_head_weights(2, 2)
+        transpose_x(0, 2)
+        quantise_hidden_weights(0)
+        scalar_regroups(1)
+        transpose_x(2, 2)
+        vector_regroups(1)
+        transpose_x(STATE, 1)
+        quantise_x(0, 2)
+        hidden_passes(0)
+        quantise_hidden_weights(1)
+        hidden_passes(1)
+        scalar_regroups(2)
+        vector_regroups(2)
+        quantise_x(2, 2)
+        bias_and_relu(0)
+        quantise_x(STATE, 1)
+        quantise_hidden_weights(2)
+        hidden_passes(2)
+        scalar_regroups(3)
+        vector_regroups(3)
+        regroup_hidden(0)
+        bias_and_relu(1)
+        quantise_hidden_weights(3)
+        quantise_hidden(0)
+        hidden_passes(3)
+        action_heads(0)
+        nc.tensor.matmul(
+            beta[:].rearrange("r a s -> r (a s)"),
+            lhsT=bias_weight[:],
+            rhs=bias_rows[:].rearrange("k a s -> k (a s)"),
+            start=True,
+            stop=True,
         )
-        nc.sync.dma_start(out=out, in_=result[:])
+        scalar_regroups(STATE)
+        vector_regroups(STATE)
+        regroup_hidden(1)
+        bias_and_relu(2)
+        quantise_hidden_weights(STATE)
+        quantise_hidden(1)
+        hidden_passes(STATE)
+        action_heads(1)
+        regroup_hidden(2)
+        bias_and_relu(3)
+        regroup_hidden(3)
+        bias_and_relu(STATE)
+        quantise_hidden(2)
+        quantise_hidden(3)
+        action_heads(2)
+        action_heads(3)
+        regroup_head_weights(STATE, nc.scalar.copy)
+        regroup_hidden(STATE)
+        quantise_head_weights(STATE, 1)
+        quantise_hidden(STATE)
+        nc.scalar.activation(out=minus_mean[:], in_=adv_sum[:], func=COPY, scale=-1.0 / A)
+        nc.vector.tensor_tensor(
+            out=base[:], in0=beta[:], in1=minus_mean[:].unsqueeze(1).to_broadcast([P, A, S]), op=ADD
+        )
+        for a in range(A):
+            head_pass(STATE, heads[a][:], False, True)
+        for a in range(A):
+            nc.vector.tensor_tensor(out=result[:, a, :], in0=heads[a][:], in1=base[:, a, :], op=ADD)
+            if a % 2:
+                pair = slice(a - 1, a + 1)
+                (nc.sync if a == A - 1 else nc.scalar).dma_start(out=out[:, pair, :], in_=result[:, pair, :])

@@ -46,7 +46,7 @@ def tile_psicritic_pa_s_kernel(tc, h1, W2, b2, W3, b3, g1, V2, c2, V3, c3, out):
 
         bh = keep.tile([P, NETS, BLOCK], BF16)
 
-        hid = keep.tile([P, NETS, 2, B, 2], BF16)
+        hid = keep.tile([P, NETS, PACK, B], BF16)
         hid_grouped = keep.tile([P, NETS, B, PACK], BF16, align_bytes=64)
         hid_codes = keep.tile([P, NETS, B], U32, align_bytes=64)
         hid_scales = keep.tile([P, NETS, B], U8, align_bytes=64)
@@ -187,16 +187,13 @@ def tile_psicritic_pa_s_kernel(tc, h1, W2, b2, W3, b3, g1, V2, c2, V3, c3, out):
         def bias_and_relu(n):
             for j in range(PACK):
                 nc.scalar.activation(
-                    out=hid[:, n, j // 2, :, j % 2],
-                    in_=sums[n][:, j, :],
-                    func=RELU,
-                    bias=bh[:, n, j : j + 1],
+                    out=hid[:, n, j, :], in_=sums[n][:, j, :], func=RELU, bias=bh[:, n, j : j + 1]
                 )
 
         def regroup_hidden(n):
             nc.vector.tensor_copy(
-                out=hid_grouped[:, n].rearrange("m r j -> m (r j)").bitcast(F32).rearrange("m (r h) -> m r h", h=2),
-                in_=hid[:, n].rearrange("m h r e -> m (h r e)").bitcast(F32).rearrange("m (h r) -> m r h", h=2),
+                out=hid_grouped[:, n].rearrange("m (c i) j -> m c j i", i=4),
+                in_=hid[:, n].rearrange("m j (c i) -> m c j i", i=4),
             )
 
         def quantise_hidden(n):

@@ -9,8 +9,8 @@ U32 = mybir.dt.uint32
 U8 = mybir.dt.uint8
 FP8X4 = mybir.dt.float8_e4m3fn_x4
 ADD = mybir.AluOpType.add
+MULT = mybir.AluOpType.mult
 RELU = mybir.ActivationFunctionType.Relu
-COPY = mybir.ActivationFunctionType.Copy
 
 P = 128
 PACK = 4
@@ -60,7 +60,6 @@ def tile_psicritic_pa_s_kernel(tc, h1, W2, b2, W3, b3, g1, V2, c2, V3, c3, out):
         bias_rows = keep.tile([P, A, S], BF16)
         bias_weight = keep.tile([P, P], BF16)
         warm = keep.tile([P, 1], F32)
-        minus_mean = keep.tile([P, S], F32)
         base = keep.tile([P, A, S], F32)
         result = keep.tile([P, A, S], F32)
 
@@ -141,17 +140,17 @@ def tile_psicritic_pa_s_kernel(tc, h1, W2, b2, W3, b3, g1, V2, c2, V3, c3, out):
             target = wh_grouped[:, n].rearrange("q j m t -> q m t j")
             copy(out=target[:, units], in_=source[:, units])
 
-        def vector_regroups(n):
-            regroup_hidden_weights(n, nc.vector.tensor_copy, slice(0, VECTOR_UNITS))
+        def vector_regroups(n, units=VECTOR_UNITS):
+            regroup_hidden_weights(n, nc.vector.tensor_copy, slice(0, units))
 
-        def scalar_regroups(n):
-            regroup_hidden_weights(n, nc.scalar.copy, slice(VECTOR_UNITS, P))
+        def scalar_regroups(n, units=VECTOR_UNITS):
+            regroup_hidden_weights(n, nc.scalar.copy, slice(units, P))
 
-        def quantise_hidden_weights(n):
+        def quantise_hidden_weights(n, parts=slice(0, PACK)):
             nc.vector.quantize_mx(
-                out=wh_codes[:, n].rearrange("q j m -> q (j m)").bitcast(FP8X4),
-                scales=wh_scales[:, n].rearrange("q j m -> q (j m)"),
-                in_=wh_grouped[:, n].rearrange("q j m t -> q (j m t)"),
+                out=wh_codes[:, n, parts].rearrange("q j m -> q (j m)").bitcast(FP8X4),
+                scales=wh_scales[:, n, parts].rearrange("q j m -> q (j m)"),
+                in_=wh_grouped[:, n, parts].rearrange("q j m t -> q (j m t)"),
             )
 
         def regroup_head_weights(n, copy):
@@ -170,9 +169,12 @@ def tile_psicritic_pa_s_kernel(tc, h1, W2, b2, W3, b3, g1, V2, c2, V3, c3, out):
 
         sums = {}
 
-        def hidden_passes(n):
-            acc = psum_acc.tile([P, PACK, B], F32, tag="acc")
-            for j in range(PACK):
+        def hidden_passes(n, parts=range(PACK)):
+            if parts[0] == 0:
+                acc = psum_acc.tile([P, PACK, B], F32, tag="acc")
+                sums[n] = acc
+            acc = sums[n]
+            for j in parts:
                 nc.tensor.matmul_mx(
                     out=acc[:, j, :],
                     lhsT=wh_codes[:, n, j, :].bitcast(FP8X4),
@@ -182,10 +184,9 @@ def tile_psicritic_pa_s_kernel(tc, h1, W2, b2, W3, b3, g1, V2, c2, V3, c3, out):
                     start=True,
                     stop=True,
                 )
-            sums[n] = acc
 
-        def bias_and_relu(n):
-            for j in range(PACK):
+        def bias_and_relu(n, parts=range(PACK)):
+            for j in parts:
                 nc.scalar.activation(
                     out=hid[:, n, j, :], in_=sums[n][:, j, :], func=RELU, bias=bh[:, n, j : j + 1]
                 )
@@ -268,13 +269,16 @@ def tile_psicritic_pa_s_kernel(tc, h1, W2, b2, W3, b3, g1, V2, c2, V3, c3, out):
         vector_regroups(STATE)
         regroup_hidden(1)
         bias_and_relu(2)
-        quantise_hidden_weights(STATE)
-        quantise_hidden(1)
-        hidden_passes(STATE)
-        action_heads(1)
+        quantise_hidden_weights(STATE, slice(0, 2))
+        hidden_passes(STATE, range(0, 2))
+        quantise_hidden_weights(STATE, slice(2, 4))
+        hidden_passes(STATE, range(2, 4))
         regroup_hidden(2)
+        quantise_hidden(1)
         bias_and_relu(3)
+        action_heads(1)
         regroup_hidden(3)
+        nc.scalar.copy(out=base[:], in_=beta[:])
         bias_and_relu(STATE)
         quantise_hidden(2)
         quantise_hidden(3)
@@ -284,9 +288,13 @@ def tile_psicritic_pa_s_kernel(tc, h1, W2, b2, W3, b3, g1, V2, c2, V3, c3, out):
         regroup_hidden(STATE)
         quantise_head_weights(STATE, 1)
         quantise_hidden(STATE)
-        nc.scalar.activation(out=minus_mean[:], in_=adv_sum[:], func=COPY, scale=-1.0 / A)
-        nc.vector.tensor_tensor(
-            out=base[:], in0=beta[:], in1=minus_mean[:].unsqueeze(1).to_broadcast([P, A, S]), op=ADD
+        nc.vector.scalar_tensor_tensor(
+            out=base[:],
+            in0=adv_sum[:].unsqueeze(1).to_broadcast([P, A, S]),
+            scalar=-1.0 / A,
+            in1=base[:],
+            op0=MULT,
+            op1=ADD,
         )
         for a in range(A):
             head_pass(STATE, heads[a][:], False, True)

@@ -20,7 +20,7 @@ F = 512
 S = 128
 NETS = A + 1
 STATE = A
-VECTOR_UNITS = 80
+VECTOR_UNITS = 88
 BLOCK = 16
 
 FLOPS = 2 * NETS * B * F * (F + S)
@@ -31,7 +31,7 @@ def tile_psicritic_pa_s_kernel(tc, h1, W2, b2, W3, b3, g1, V2, c2, V3, c3, out):
     with ExitStack() as ctx:
         keep = ctx.enter_context(tc.tile_pool(name="keep", bufs=1))
         psum_small = ctx.enter_context(tc.psum_pool(name="psum_small", bufs=4))
-        psum_acc = ctx.enter_context(tc.psum_pool(name="psum_acc", bufs=2))
+        psum_acc = ctx.enter_context(tc.psum_pool(name="psum_acc", bufs=3))
         psum_one = ctx.enter_context(tc.psum_pool(name="psum_one", bufs=1))
 
         x_rows = keep.tile([P, NETS, F], BF16)
@@ -98,8 +98,6 @@ def tile_psicritic_pa_s_kernel(tc, h1, W2, b2, W3, b3, g1, V2, c2, V3, c3, out):
                 out=x_rows[:, first : first + count, :], in_=h1[:, first : first + count, :]
             )
 
-        load_head_weights(0, 1)
-        load_head_weights(1, 3)
         load_hidden_weights(0)
         load_x(0, 2)
         load_hidden_weights(1)
@@ -107,11 +105,13 @@ def tile_psicritic_pa_s_kernel(tc, h1, W2, b2, W3, b3, g1, V2, c2, V3, c3, out):
         nc.sync.dma_start(out=x_rows[:, STATE, :], in_=g1)
         load_hidden_weights(2)
         load_hidden_weights(3)
+        load_hidden_weights(STATE)
+        load_head_weights(0, 2)
+        load_head_weights(2, 2)
         nc.sync.dma_start(
             out=wo_rows[:, STATE].rearrange("m j s -> m (j s)"),
             in_=V3.rearrange("(m j) s -> m (j s)", j=PACK),
         )
-        load_hidden_weights(STATE)
 
         def transpose_x(first, count):
             xt = psum_small.tile([P, count, 2, B], F32, tag="small")
@@ -215,8 +215,6 @@ def tile_psicritic_pa_s_kernel(tc, h1, W2, b2, W3, b3, g1, V2, c2, V3, c3, out):
                 stop=stop,
             )
 
-        adv_sum = psum_one.tile([P, S], F32)
-        beta = psum_one.tile([P, A, S], F32)
         heads = {}
 
         def action_heads(a):
@@ -225,19 +223,23 @@ def tile_psicritic_pa_s_kernel(tc, h1, W2, b2, W3, b3, g1, V2, c2, V3, c3, out):
             head_pass(a, adv_sum[:], a == 0, a == A - 1)
             head_pass(a, heads[a][:], True, False)
 
-        regroup_head_weights(0, nc.vector.tensor_copy)
-        regroup_head_weights(1, nc.vector.tensor_copy)
-        regroup_head_weights(2, nc.vector.tensor_copy)
-        regroup_head_weights(3, nc.vector.tensor_copy)
-        quantise_head_weights(0, 2)
+        beta = psum_one.tile([P, A, S], F32, tag="one")
+        nc.tensor.matmul(
+            beta[:].rearrange("r a s -> r (a s)"),
+            lhsT=bias_weight[:],
+            rhs=bias_rows[:].rearrange("k a s -> k (a s)"),
+            start=True,
+            stop=True,
+        )
         scalar_regroups(0)
+        nc.scalar.copy(out=base[:], in_=beta[:])
+        adv_sum = psum_one.tile([P, S], F32, tag="one")
         vector_regroups(0)
-        quantise_head_weights(2, 2)
         transpose_x(0, 2)
         quantise_hidden_weights(0)
         scalar_regroups(1)
-        transpose_x(2, 2)
         vector_regroups(1)
+        transpose_x(2, 2)
         transpose_x(STATE, 1)
         quantise_x(0, 2)
         hidden_passes(0)
@@ -246,8 +248,8 @@ def tile_psicritic_pa_s_kernel(tc, h1, W2, b2, W3, b3, g1, V2, c2, V3, c3, out):
         scalar_regroups(2)
         vector_regroups(2)
         quantise_x(2, 2)
-        bias_and_relu(0)
         quantise_x(STATE, 1)
+        bias_and_relu(0)
         quantise_hidden_weights(2)
         hidden_passes(2)
         scalar_regroups(3)
@@ -255,36 +257,32 @@ def tile_psicritic_pa_s_kernel(tc, h1, W2, b2, W3, b3, g1, V2, c2, V3, c3, out):
         regroup_hidden(0)
         bias_and_relu(1)
         quantise_hidden_weights(3)
-        quantise_hidden(0)
         hidden_passes(3)
-        action_heads(0)
-        nc.tensor.matmul(
-            beta[:].rearrange("r a s -> r (a s)"),
-            lhsT=bias_weight[:],
-            rhs=bias_rows[:].rearrange("k a s -> k (a s)"),
-            start=True,
-            stop=True,
-        )
+        quantise_hidden(0)
         scalar_regroups(STATE)
         vector_regroups(STATE)
         regroup_hidden(1)
         bias_and_relu(2)
-        quantise_hidden_weights(STATE, slice(0, 2))
-        hidden_passes(STATE, range(0, 2))
-        quantise_hidden_weights(STATE, slice(2, 4))
-        hidden_passes(STATE, range(2, 4))
-        regroup_hidden(2)
+        quantise_hidden_weights(STATE)
+        hidden_passes(STATE)
+        regroup_head_weights(0, nc.scalar.copy)
+        regroup_head_weights(1, nc.scalar.copy)
         quantise_hidden(1)
+        regroup_hidden(2)
         bias_and_relu(3)
-        action_heads(1)
+        regroup_head_weights(3, nc.vector.tensor_copy)
         regroup_hidden(3)
-        nc.scalar.copy(out=base[:], in_=beta[:])
-        bias_and_relu(STATE)
         quantise_hidden(2)
+        regroup_head_weights(2, nc.scalar.copy)
+        bias_and_relu(STATE)
+        quantise_head_weights(0, 2)
         quantise_hidden(3)
+        action_heads(0)
+        action_heads(1)
+        regroup_head_weights(STATE, nc.scalar.copy)
+        quantise_head_weights(2, 2)
         action_heads(2)
         action_heads(3)
-        regroup_head_weights(STATE, nc.scalar.copy)
         regroup_hidden(STATE)
         quantise_head_weights(STATE, 1)
         quantise_hidden(STATE)

@@ -70,16 +70,16 @@ def tile_psicritic_pa_s_kernel(tc, h1, W2, b2, W3, b3, g1, V2, c2, V3, c3, out):
         nc.vector.memset(bias_rows[:], 0.0)
         nc.scalar.dma_start(out=bh[:, 0:A, 0:PACK], in_=b2.rearrange("a (m j) -> m a j", j=PACK))
         nc.scalar.dma_start(out=bh[:, STATE, 0:PACK], in_=c2.rearrange("(m j) -> m j", j=PACK))
-        nc.scalar.dma_start(out=bias_rows[0:1, :, :], in_=b3.rearrange("(o a) s -> o a s", o=1))
-        nc.scalar.dma_start(
-            out=bias_rows[1:2, :, :],
-            in_=c3.rearrange("(o r s) -> o r s", o=1, r=1).to_broadcast([1, A, S]),
-        )
-        nc.scalar.dma_start(out=bias_rows[32:36, :, :], in_=b3.unsqueeze(1).to_broadcast([A, A, S]))
         nc.scalar.activation(out=warm[:], in_=warm[:], func=RELU)
         nc.vector.memset(bias_weight[:], 1.0)
         nc.vector.memset(bias_weight[32:64, :], -1.0 / A)
         make_identity(nc, identity[:])
+        nc.gpsimd.dma_start(out=bias_rows[0:1, :, :], in_=b3.rearrange("(o a) s -> o a s", o=1))
+        nc.gpsimd.dma_start(
+            out=bias_rows[1:2, :, :],
+            in_=c3.rearrange("(o r s) -> o r s", o=1, r=1).to_broadcast([1, A, S]),
+        )
+        nc.gpsimd.dma_start(out=bias_rows[32:36, :, :], in_=b3.unsqueeze(1).to_broadcast([A, A, S]))
 
         def load_hidden_weights(n):
             nc.sync.dma_start(
@@ -224,16 +224,7 @@ def tile_psicritic_pa_s_kernel(tc, h1, W2, b2, W3, b3, g1, V2, c2, V3, c3, out):
             head_pass(a, heads[a][:], True, False)
 
         beta = psum_one.tile([P, A, S], F32, tag="one")
-        nc.tensor.matmul(
-            beta[:].rearrange("r a s -> r (a s)"),
-            lhsT=bias_weight[:],
-            rhs=bias_rows[:].rearrange("k a s -> k (a s)"),
-            start=True,
-            stop=True,
-        )
         scalar_regroups(0)
-        nc.scalar.copy(out=base[:], in_=beta[:])
-        adv_sum = psum_one.tile([P, S], F32, tag="one")
         vector_regroups(0)
         transpose_x(0, 2)
         quantise_hidden_weights(0)
@@ -265,16 +256,25 @@ def tile_psicritic_pa_s_kernel(tc, h1, W2, b2, W3, b3, g1, V2, c2, V3, c3, out):
         bias_and_relu(2)
         quantise_hidden_weights(STATE)
         hidden_passes(STATE)
+        nc.tensor.matmul(
+            beta[:].rearrange("r a s -> r (a s)"),
+            lhsT=bias_weight[:],
+            rhs=bias_rows[:].rearrange("k a s -> k (a s)"),
+            start=True,
+            stop=True,
+        )
         regroup_head_weights(0, nc.scalar.copy)
         regroup_head_weights(1, nc.scalar.copy)
         quantise_hidden(1)
         regroup_hidden(2)
         bias_and_relu(3)
-        regroup_head_weights(3, nc.vector.tensor_copy)
+        regroup_head_weights(2, nc.vector.tensor_copy)
         regroup_hidden(3)
+        regroup_head_weights(3, nc.vector.tensor_copy)
         quantise_hidden(2)
-        regroup_head_weights(2, nc.scalar.copy)
         bias_and_relu(STATE)
+        nc.scalar.copy(out=base[:], in_=beta[:])
+        adv_sum = psum_one.tile([P, S], F32, tag="one")
         quantise_head_weights(0, 2)
         quantise_hidden(3)
         action_heads(0)

@@ -31,7 +31,7 @@ def tile_psicritic_pa_s_kernel(tc, h1, W2, b2, W3, b3, g1, V2, c2, V3, c3, out):
     with ExitStack() as ctx:
         keep = ctx.enter_context(tc.tile_pool(name="keep", bufs=1))
         psum_small = ctx.enter_context(tc.psum_pool(name="psum_small", bufs=4))
-        psum_acc = ctx.enter_context(tc.psum_pool(name="psum_acc", bufs=3))
+        psum_acc = ctx.enter_context(tc.psum_pool(name="psum_acc", bufs=2))
         psum_one = ctx.enter_context(tc.psum_pool(name="psum_one", bufs=1))
 
         x_rows = keep.tile([P, NETS, F], BF16)
@@ -74,12 +74,6 @@ def tile_psicritic_pa_s_kernel(tc, h1, W2, b2, W3, b3, g1, V2, c2, V3, c3, out):
         nc.vector.memset(bias_weight[:], 1.0)
         nc.vector.memset(bias_weight[32:64, :], -1.0 / A)
         make_identity(nc, identity[:])
-        nc.gpsimd.dma_start(out=bias_rows[0:1, :, :], in_=b3.rearrange("(o a) s -> o a s", o=1))
-        nc.gpsimd.dma_start(
-            out=bias_rows[1:2, :, :],
-            in_=c3.rearrange("(o r s) -> o r s", o=1, r=1).to_broadcast([1, A, S]),
-        )
-        nc.gpsimd.dma_start(out=bias_rows[32:36, :, :], in_=b3.unsqueeze(1).to_broadcast([A, A, S]))
 
         def load_hidden_weights(n):
             nc.sync.dma_start(
@@ -112,6 +106,13 @@ def tile_psicritic_pa_s_kernel(tc, h1, W2, b2, W3, b3, g1, V2, c2, V3, c3, out):
             out=wo_rows[:, STATE].rearrange("m j s -> m (j s)"),
             in_=V3.rearrange("(m j) s -> m (j s)", j=PACK),
         )
+
+        nc.sync.dma_start(out=bias_rows[0:1, :, :], in_=b3.rearrange("(o a) s -> o a s", o=1))
+        nc.sync.dma_start(
+            out=bias_rows[1:2, :, :],
+            in_=c3.rearrange("(o r s) -> o r s", o=1, r=1).to_broadcast([1, A, S]),
+        )
+        nc.sync.dma_start(out=bias_rows[32:36, :, :], in_=b3.unsqueeze(1).to_broadcast([A, A, S]))
 
         def transpose_x(first, count):
             xt = psum_small.tile([P, count, 2, B], F32, tag="small")
@@ -215,6 +216,8 @@ def tile_psicritic_pa_s_kernel(tc, h1, W2, b2, W3, b3, g1, V2, c2, V3, c3, out):
                 stop=stop,
             )
 
+        adv_sum = psum_one.tile([P, S], F32)
+        beta = psum_one.tile([P, A, S], F32)
         heads = {}
 
         def action_heads(a):
@@ -223,7 +226,6 @@ def tile_psicritic_pa_s_kernel(tc, h1, W2, b2, W3, b3, g1, V2, c2, V3, c3, out):
             head_pass(a, adv_sum[:], a == 0, a == A - 1)
             head_pass(a, heads[a][:], True, False)
 
-        beta = psum_one.tile([P, A, S], F32, tag="one")
         scalar_regroups(0)
         vector_regroups(0)
         transpose_x(0, 2)
@@ -273,13 +275,12 @@ def tile_psicritic_pa_s_kernel(tc, h1, W2, b2, W3, b3, g1, V2, c2, V3, c3, out):
         regroup_head_weights(3, nc.vector.tensor_copy)
         quantise_hidden(2)
         bias_and_relu(STATE)
+        regroup_head_weights(STATE, nc.scalar.copy)
         nc.scalar.copy(out=base[:], in_=beta[:])
-        adv_sum = psum_one.tile([P, S], F32, tag="one")
         quantise_head_weights(0, 2)
         quantise_hidden(3)
         action_heads(0)
         action_heads(1)
-        regroup_head_weights(STATE, nc.scalar.copy)
         quantise_head_weights(2, 2)
         action_heads(2)
         action_heads(3)

@@ -20,7 +20,7 @@ F = 512
 S = 128
 NETS = A + 1
 STATE = A
-VECTOR_UNITS = 88
+VECTOR_UNITS = 96
 BLOCK = 16
 
 FLOPS = 2 * NETS * B * F * (F + S)
@@ -66,10 +66,7 @@ def tile_psicritic_pa_s_kernel(tc, h1, W2, b2, W3, b3, g1, V2, c2, V3, c3, out):
         ctx.enter_context(tc.manual_schedule())
 
         nc.vector.memset(warm[:], 0.0)
-
         nc.vector.memset(bias_rows[:], 0.0)
-        nc.scalar.dma_start(out=bh[:, 0:A, 0:PACK], in_=b2.rearrange("a (m j) -> m a j", j=PACK))
-        nc.scalar.dma_start(out=bh[:, STATE, 0:PACK], in_=c2.rearrange("(m j) -> m j", j=PACK))
         nc.scalar.activation(out=warm[:], in_=warm[:], func=RELU)
         nc.vector.memset(bias_weight[:], 1.0)
         nc.vector.memset(bias_weight[32:64, :], -1.0 / A)
@@ -95,6 +92,8 @@ def tile_psicritic_pa_s_kernel(tc, h1, W2, b2, W3, b3, g1, V2, c2, V3, c3, out):
         load_hidden_weights(0)
         load_x(0, 2)
         load_hidden_weights(1)
+        nc.sync.dma_start(out=bh[:, 0:A, 0:PACK], in_=b2.rearrange("a (m j) -> m a j", j=PACK))
+        nc.sync.dma_start(out=bh[:, STATE, 0:PACK], in_=c2.rearrange("(m j) -> m j", j=PACK))
         load_x(2, 2)
         nc.sync.dma_start(out=x_rows[:, STATE, :], in_=g1)
         load_hidden_weights(2)
@@ -251,13 +250,6 @@ def tile_psicritic_pa_s_kernel(tc, h1, W2, b2, W3, b3, g1, V2, c2, V3, c3, out):
         bias_and_relu(1)
         quantise_hidden_weights(3)
         hidden_passes(3)
-        quantise_hidden(0)
-        scalar_regroups(STATE)
-        vector_regroups(STATE)
-        regroup_hidden(1)
-        bias_and_relu(2)
-        quantise_hidden_weights(STATE)
-        hidden_passes(STATE)
         nc.tensor.matmul(
             beta[:].rearrange("r a s -> r (a s)"),
             lhsT=bias_weight[:],
@@ -265,6 +257,13 @@ def tile_psicritic_pa_s_kernel(tc, h1, W2, b2, W3, b3, g1, V2, c2, V3, c3, out):
             start=True,
             stop=True,
         )
+        quantise_hidden(0)
+        scalar_regroups(STATE)
+        vector_regroups(STATE)
+        regroup_hidden(1)
+        bias_and_relu(2)
+        quantise_hidden_weights(STATE)
+        hidden_passes(STATE)
         regroup_head_weights(0, nc.scalar.copy)
         regroup_head_weights(1, nc.scalar.copy)
         quantise_hidden(1)
@@ -272,11 +271,11 @@ def tile_psicritic_pa_s_kernel(tc, h1, W2, b2, W3, b3, g1, V2, c2, V3, c3, out):
         bias_and_relu(3)
         regroup_head_weights(2, nc.vector.tensor_copy)
         regroup_hidden(3)
-        regroup_head_weights(3, nc.vector.tensor_copy)
+        nc.scalar.copy(out=base[:], in_=beta[:])
+        regroup_head_weights(3, nc.scalar.copy)
         quantise_hidden(2)
         bias_and_relu(STATE)
         regroup_head_weights(STATE, nc.scalar.copy)
-        nc.scalar.copy(out=base[:], in_=beta[:])
         quantise_head_weights(0, 2)
         quantise_hidden(3)
         action_heads(0)

from contextlib import ExitStack

import concourse.mybir as mybir
from concourse.masks import make_identity

F32 = mybir.dt.float32
BF16 = mybir.dt.bfloat16
U32 = mybir.dt.uint32
U8 = mybir.dt.uint8
FP8X4 = mybir.dt.float8_e4m3fn_x4
ADD = mybir.AluOpType.add
MULT = mybir.AluOpType.mult
RELU = mybir.ActivationFunctionType.Relu

P = 128
PACK = 4
B = 128
A = 4
F = 512
S = 128
NETS = A + 1
STATE = A
VECTOR_UNITS = 96
BLOCK = 16

FLOPS = 2 * NETS * B * F * (F + S)


def tile_psicritic_pa_s_kernel(tc, h1, W2, b2, W3, b3, g1, V2, c2, V3, c3, out):
    nc = tc.nc
    with ExitStack() as ctx:
        keep = ctx.enter_context(tc.tile_pool(name="keep", bufs=1))
        psum_small = ctx.enter_context(tc.psum_pool(name="psum_small", bufs=4))
        psum_acc = ctx.enter_context(tc.psum_pool(name="psum_acc", bufs=2))
        psum_one = ctx.enter_context(tc.psum_pool(name="psum_one", bufs=1))

        x_rows = keep.tile([P, NETS, F], BF16)
        x_grouped = keep.tile([P, NETS, B, PACK], BF16, align_bytes=64)
        x_codes = keep.tile([P, NETS, B], U32, align_bytes=64)
        x_scales = keep.tile([P, NETS, B], U8, align_bytes=64)

        wh_rows = keep.tile([P, NETS, PACK, F], BF16)
        wh_grouped = keep.tile([P, NETS, PACK, P, PACK], BF16, align_bytes=64)
        wh_codes = keep.tile([P, NETS, PACK, P], U32, align_bytes=64)
        wh_scales = keep.tile([P, NETS, PACK, P], U8, align_bytes=64)

        bh = keep.tile([P, NETS, BLOCK], BF16)

        hid = keep.tile([P, NETS, PACK, B], BF16)
        hid_grouped = keep.tile([P, NETS, B, PACK], BF16, align_bytes=64)
        hid_codes = keep.tile([P, NETS, B], U32, align_bytes=64)
        hid_scales = keep.tile([P, NETS, B], U8, align_bytes=64)

        wo_rows = keep.tile([P, NETS, PACK, S], BF16)
        wo_grouped = keep.tile([P, NETS, S, PACK], BF16, align_bytes=64)
        wo_codes = keep.tile([P, NETS, S], U32, align_bytes=64)
        wo_scales = keep.tile([P, NETS, S], U8, align_bytes=64)

        identity = keep.tile([P, P], F32)
        bias_rows = keep.tile([P, A, S], BF16)
        bias_weight = keep.tile([P, P], BF16)
        warm = keep.tile([P, 1], F32)
        base = keep.tile([P, A, S], F32)
        result = keep.tile([P, A, S], F32)

        ctx.enter_context(tc.manual_schedule())

        nc.vector.memset(warm[:], 0.0)
        nc.vector.memset(bias_rows[:], 0.0)
        nc.scalar.activation(out=warm[:], in_=warm[:], func=RELU)
        nc.vector.memset(bias_weight[:], 1.0)
        nc.vector.memset(bias_weight[32:64, :], -1.0 / A)
        make_identity(nc, identity[:])

        def load_hidden_weights(n):
            nc.sync.dma_start(
                out=wh_rows[:, n].rearrange("q t f -> q (t f)"),
                in_=(V2 if n == STATE else W2[n]).rearrange("(q t) f -> q (t f)", t=PACK),
            )

        def load_head_weights(first, count):
            nc.sync.dma_start(
                out=wo_rows[:, first : first + count].rearrange("m a j s -> m a (j s)"),
                in_=W3[first : first + count].rearrange("a (m j) s -> m a (j s)", j=PACK),
            )

        def load_x(first, count):
            nc.sync.dma_start(
                out=x_rows[:, first : first + count, :], in_=h1[:, first : first + count, :]
            )

        load_hidden_weights(0)
        load_x(0, 2)
        load_hidden_weights(1)
        nc.sync.dma_start(out=bh[:, 0:A, 0:PACK], in_=b2.rearrange("a (m j) -> m a j", j=PACK))
        nc.sync.dma_start(out=bh[:, STATE, 0:PACK], in_=c2.rearrange("(m j) -> m j", j=PACK))
        load_x(2, 2)
        nc.sync.dma_start(out=x_rows[:, STATE, :], in_=g1)
        load_hidden_weights(2)
        load_hidden_weights(3)
        load_hidden_weights(STATE)
        load_head_weights(0, 2)
        load_head_weights(2, 2)
        nc.sync.dma_start(
            out=wo_rows[:, STATE].rearrange("m j s -> m (j s)"),
            in_=V3.rearrange("(m j) s -> m (j s)", j=PACK),
        )

        nc.sync.dma_start(out=bias_rows[0:1, :, :], in_=b3.rearrange("(o a) s -> o a s", o=1))
        nc.sync.dma_start(
            out=bias_rows[1:2, :, :],
            in_=c3.rearrange("(o r s) -> o r s", o=1, r=1).to_broadcast([1, A, S]),
        )
        nc.sync.dma_start(out=bias_rows[32:36, :, :], in_=b3.unsqueeze(1).to_broadcast([A, A, S]))

        def transpose_x(first, count):
            xt = psum_small.tile([P, count, 2, B], F32, tag="small")
            for i in range(count):
                words = x_rows[:, first + i, :].bitcast(F32)
                for u in range(2):
                    nc.tensor.transpose(xt[:, i, u, :], words[:, u::2], identity[:])
            nc.scalar.copy(
                out=x_grouped[:, first : first + count]
                .rearrange("q n r t -> q (n r t)")
                .bitcast(F32)
                .rearrange("q (n r u) -> q n r u", n=count, u=2),
                in_=xt[:].rearrange("q n u r -> q n r u"),
            )

        def quantise_x(first, count):
            nets = slice(first, first + count)
            nc.vector.quantize_mx(
                out=x_codes[:, nets, :].rearrange("q n r -> q (n r)").bitcast(FP8X4),
                scales=x_scales[:, nets, :].rearrange("q n r -> q (n r)"),
                in_=x_grouped[:, nets].rearrange("q n r t -> q (n r t)"),
            )

        def regroup_hidden_weights(n, copy, units):
            source = wh_rows[:, n].rearrange("q t (m j) -> q m t j", j=PACK)
            target = wh_grouped[:, n].rearrange("q j m t -> q m t j")
            copy(out=target[:, units], in_=source[:, units])

        def vector_regroups(n, units=VECTOR_UNITS):
            regroup_hidden_weights(n, nc.vector.tensor_copy, slice(0, units))

        def scalar_regroups(n, units=VECTOR_UNITS):
            regroup_hidden_weights(n, nc.scalar.copy, slice(units, P))

        def quantise_hidden_weights(n, parts=slice(0, PACK)):
            nc.vector.quantize_mx(
                out=wh_codes[:, n, parts].rearrange("q j m -> q (j m)").bitcast(FP8X4),
                scales=wh_scales[:, n, parts].rearrange("q j m -> q (j m)"),
                in_=wh_grouped[:, n, parts].rearrange("q j m t -> q (j m t)"),
            )

        def regroup_head_weights(n, copy):
            copy(
                out=wo_grouped[:, n].rearrange("m (c i) j -> m c j i", i=4),
                in_=wo_rows[:, n].rearrange("m j (c i) -> m c j i", i=4),
            )

        def quantise_head_weights(first, count):
            nets = slice(first, first + count)
            nc.vector.quantize_mx(
                out=wo_codes[:, nets, :].rearrange("m n s -> m (n s)").bitcast(FP8X4),
                scales=wo_scales[:, nets, :].rearrange("m n s -> m (n s)"),
                in_=wo_grouped[:, nets].rearrange("m n s j -> m (n s j)"),
            )

        sums = {}

        def hidden_passes(n, parts=range(PACK)):
            if parts[0] == 0:
                acc = psum_acc.tile([P, PACK, B], F32, tag="acc")
                sums[n] = acc
            acc = sums[n]
            for j in parts:
                nc.tensor.matmul_mx(
                    out=acc[:, j, :],
                    lhsT=wh_codes[:, n, j, :].bitcast(FP8X4),
                    lhsT_scale=wh_scales[:, n, j, :],
                    rhs=x_codes[:, n, :].bitcast(FP8X4),
                    rhs_scale=x_scales[:, n, :],
                    start=True,
                    stop=True,
                )

        def bias_and_relu(n, parts=range(PACK)):
            for j in parts:
                nc.scalar.activation(
                    out=hid[:, n, j, :], in_=sums[n][:, j, :], func=RELU, bias=bh[:, n, j : j + 1]
                )

        def regroup_hidden(n):
            nc.vector.tensor_copy(
                out=hid_grouped[:, n].rearrange("m (c i) j -> m c j i", i=4),
                in_=hid[:, n].rearrange("m j (c i) -> m c j i", i=4),
            )

        def quantise_hidden(n):
            nc.vector.quantize_mx(
                out=hid_codes[:, n, :].bitcast(FP8X4),
                scales=hid_scales[:, n, :],
                in_=hid_grouped[:, n].rearrange("m r j -> m (r j)"),
            )

        def head_pass(n, target, start, stop):
            nc.tensor.matmul_mx(
                out=target,
                lhsT=hid_codes[:, n, :].bitcast(FP8X4),
                lhsT_scale=hid_scales[:, n, :],
                rhs=wo_codes[:, n, :].bitcast(FP8X4),
                rhs_scale=wo_scales[:, n, :],
                start=start,
                stop=stop,
            )

        adv_sum = psum_one.tile([P, S], F32)
        beta = psum_one.tile([P, A, S], F32)
        heads = {}

        def action_heads(a):
            head = psum_small.tile([P, S], F32, tag="small")
            heads[a] = head
            head_pass(a, adv_sum[:], a == 0, a == A - 1)
            head_pass(a, heads[a][:], True, False)

        scalar_regroups(0)
        vector_regroups(0)
        transpose_x(0, 2)
        quantise_hidden_weights(0)
        scalar_regroups(1)
        vector_regroups(1)
        transpose_x(2, 2)
        transpose_x(STATE, 1)
        quantise_x(0, 2)
        hidden_passes(0)
        quantise_hidden_weights(1)
        hidden_passes(1)
        scalar_regroups(2)
        vector_regroups(2)
        quantise_x(2, 2)
        quantise_x(STATE, 1)
        bias_and_relu(0)
        quantise_hidden_weights(2)
        hidden_passes(2)
        scalar_regroups(3)
        vector_regroups(3)
        regroup_hidden(0)
        bias_and_relu(1)
        quantise_hidden_weights(3)
        hidden_passes(3)
        nc.tensor.matmul(
            beta[:].rearrange("r a s -> r (a s)"),
            lhsT=bias_weight[:],
            rhs=bias_rows[:].rearrange("k a s -> k (a s)"),
            start=True,
            stop=True,
        )
        quantise_hidden(0)
        scalar_regroups(STATE)
        vector_regroups(STATE)
        regroup_hidden(1)
        bias_and_relu(2)
        quantise_hidden_weights(STATE)
        hidden_passes(STATE)
        regroup_head_weights(0, nc.scalar.copy)
        regroup_head_weights(1, nc.scalar.copy)
        quantise_hidden(1)
        regroup_hidden(2)
        bias_and_relu(3)
        regroup_head_weights(2, nc.vector.tensor_copy)
        regroup_hidden(3)
        nc.scalar.copy(out=base[:], in_=beta[:])
        regroup_head_weights(3, nc.scalar.copy)
        quantise_hidden(2)
        bias_and_relu(STATE)
        regroup_head_weights(STATE, nc.scalar.copy)
        quantise_head_weights(0, 2)
        quantise_hidden(3)
        action_heads(0)
        action_heads(1)
        quantise_head_weights(2, 2)
        action_heads(2)
        action_heads(3)
        regroup_hidden(STATE)
        quantise_head_weights(STATE, 1)
        quantise_hidden(STATE)
        nc.vector.scalar_tensor_tensor(
            out=base[:],
            in0=adv_sum[:].unsqueeze(1).to_broadcast([P, A, S]),
            scalar=-1.0 / A,
            in1=base[:],
            op0=MULT,
            op1=ADD,
        )
        for a in range(A):
            head_pass(STATE, heads[a][:], False, True)
        for a in range(A):
            nc.vector.tensor_tensor(out=result[:, a, :], in0=heads[a][:], in1=base[:, a, :], op=ADD)
            if a % 2:
                pair = slice(a - 1, a + 1)
                (nc.sync if a == A - 1 else nc.scalar).dma_start(out=out[:, pair, :], in_=result[:, pair, :])
